import numpy as np
import ml_dtypes

BF16 = ml_dtypes.bfloat16


def bf(x):
    return np.asarray(x, np.float32).astype(BF16)


def f32(x):
    return np.asarray(x, np.float32)


def f64(x):
    return np.asarray(x).astype(np.float64)


def striped(idx):
    return np.tile(idx.reshape(-1, 16).T, (8, 1))


C, D, S, N = 512, 256, 2048, 256
SCALING = 4.0


def silu(v):
    return v / (1.0 + np.exp(-v))


def setup_inputs():
    return {"base": f32(np.random.standard_normal((C, S))), "x": bf(np.random.standard_normal((D, N))), "w_gate": bf(np.random.standard_normal((D, C)) / np.sqrt(D)), "w_ad": bf(0.5 * np.random.standard_normal((D, C)) / np.sqrt(D)), "tw": f32(0.1 + 0.9 * np.random.random_sample((1, N))), "offs": striped(np.random.permutation(S)[:N])}


def reference(base, x, w_gate, w_ad, tw, offs):
    idx = offs[:16].T.reshape(-1)
    gate = silu(f64(w_gate).T @ f64(x))
    up = (f64(w_ad).T @ f64(x)) * SCALING * f64(tw)
    out = f64(base).copy()
    out[:, idx] = gate * up
    return out

@@ -1,0 +1,66 @@
+import concourse.mybir as mybir
+
+F32 = mybir.dt.float32
+BF16 = mybir.dt.bfloat16
+U16 = mybir.dt.uint16
+MULT = mybir.AluOpType.mult
+SILU = mybir.ActivationFunctionType.Silu
+
+P = 128
+C, D, S, N = 512, 256, 2048, 256
+C_BLOCKS = C // P
+D_BLOCKS = D // P
+SCALING = 4.0
+
+FLOPS = 2 * 2 * D * C * N
+
+
+def tile_feedforward_kernel(tc, base, x, w_gate, w_ad, tw, offs, out):
+    nc = tc.nc
+    with (
+        tc.tile_pool(name="held", bufs=1) as held,
+        tc.tile_pool(name="work", bufs=2) as work,
+        tc.psum_pool(name="psum", bufs=2) as psum,
+    ):
+        offsets = held.tile([P, N // 16], U16, name="offsets")
+        nc.sync.dma_start(offsets[:], offs)
+
+        x_sb = held.tile([P, D_BLOCKS, N], BF16, name="x_sb")
+        w_gate_sb = held.tile([P, D_BLOCKS, C], BF16, name="w_gate_sb")
+        w_ad_sb = held.tile([P, D_BLOCKS, C], BF16, name="w_ad_sb")
+        nc.scalar.dma_start(x_sb[:], x.rearrange("(k p) n -> p k n", p=P))
+        nc.scalar.dma_start(w_gate_sb[:], w_gate.rearrange("(k p) c -> p k c", p=P))
+        nc.scalar.dma_start(w_ad_sb[:], w_ad.rearrange("(k p) c -> p k c", p=P))
+
+        tw_sb = held.tile([P, N], F32, name="tw_sb")
+        nc.scalar.dma_start(tw_sb[:], tw.to_broadcast([P, N]))
+
+        windows = [held.tile([P, S], F32, name=f"window{cb}") for cb in range(C_BLOCKS)]
+        for cb in range(C_BLOCKS):
+            nc.sync.dma_start(windows[cb][:], base[cb * P : (cb + 1) * P, :])
+
+        for cb in range(C_BLOCKS):
+            channels = slice(cb * P, (cb + 1) * P)
+
+            gate_ps = psum.tile([P, N], F32, name="gate_ps")
+            up_ps = psum.tile([P, N], F32, name="up_ps")
+            for k in range(D_BLOCKS):
+                nc.tensor.matmul(
+                    gate_ps[:], w_gate_sb[:, k, channels], x_sb[:, k, :],
+                    start=(k == 0), stop=(k == D_BLOCKS - 1),
+                )
+            for k in range(D_BLOCKS):
+                nc.tensor.matmul(
+                    up_ps[:], w_ad_sb[:, k, channels], x_sb[:, k, :],
+                    start=(k == 0), stop=(k == D_BLOCKS - 1),
+                )
+
+            gate = work.tile([P, N], F32, name="gate")
+            nc.scalar.activation(gate[:], gate_ps[:], SILU)
+
+            up = work.tile([P, N], F32, name="up")
+            nc.vector.scalar_tensor_tensor(up[:], up_ps[:], SCALING, tw_sb[:], MULT, MULT)
+
+            nc.vector.tensor_tensor(windows[cb][:].indirect(offsets[:]), gate[:], up[:], MULT)
+
+            nc.sync.dma_start(out[channels, :], windows[cb][:])

@@ -19,8 +19,8 @@ def tile_feedforward_kernel(tc, base, x, w_gate, w_ad, tw, offs, out):
     nc = tc.nc
     with (
         tc.tile_pool(name="held", bufs=1) as held,
-        tc.tile_pool(name="work", bufs=2) as work,
-        tc.psum_pool(name="psum", bufs=2) as psum,
+        tc.tile_pool(name="work", bufs=C_BLOCKS) as work,
+        tc.psum_pool(name="psum", bufs=C_BLOCKS) as psum,
     ):
         offsets = held.tile([P, N // 16], U16, name="offsets")
         nc.sync.dma_start(offsets[:], offs)
@@ -28,12 +28,12 @@ def tile_feedforward_kernel(tc, base, x, w_gate, w_ad, tw, offs, out):
         x_sb = held.tile([P, D_BLOCKS, N], BF16, name="x_sb")
         w_gate_sb = held.tile([P, D_BLOCKS, C], BF16, name="w_gate_sb")
         w_ad_sb = held.tile([P, D_BLOCKS, C], BF16, name="w_ad_sb")
-        nc.scalar.dma_start(x_sb[:], x.rearrange("(k p) n -> p k n", p=P))
-        nc.scalar.dma_start(w_gate_sb[:], w_gate.rearrange("(k p) c -> p k c", p=P))
-        nc.scalar.dma_start(w_ad_sb[:], w_ad.rearrange("(k p) c -> p k c", p=P))
+        nc.sync.dma_start(x_sb[:], x.rearrange("(k p) n -> p k n", p=P))
+        nc.sync.dma_start(w_gate_sb[:], w_gate.rearrange("(k p) c -> p k c", p=P))
+        nc.sync.dma_start(w_ad_sb[:], w_ad.rearrange("(k p) c -> p k c", p=P))
 
         tw_sb = held.tile([P, N], F32, name="tw_sb")
-        nc.scalar.dma_start(tw_sb[:], tw.to_broadcast([P, N]))
+        nc.sync.dma_start(tw_sb[:], tw.to_broadcast([P, N]))
 
         windows = [held.tile([P, S], F32, name=f"window{cb}") for cb in range(C_BLOCKS)]
         for cb in range(C_BLOCKS):

@@ -17,10 +17,10 @@ FLOPS = 2 * 2 * D * C * N
 
 def tile_feedforward_kernel(tc, base, x, w_gate, w_ad, tw, offs, out):
     nc = tc.nc
+    queues = [nc.sync, nc.scalar]
     with (
         tc.tile_pool(name="held", bufs=1) as held,
-        tc.tile_pool(name="work", bufs=C_BLOCKS) as work,
-        tc.psum_pool(name="psum", bufs=C_BLOCKS) as psum,
+        tc.psum_pool(name="psum", bufs=1) as psum,
     ):
         offsets = held.tile([P, N // 16], U16, name="offsets")
         nc.sync.dma_start(offsets[:], offs)
@@ -28,22 +28,23 @@ def tile_feedforward_kernel(tc, base, x, w_gate, w_ad, tw, offs, out):
         x_sb = held.tile([P, D_BLOCKS, N], BF16, name="x_sb")
         w_gate_sb = held.tile([P, D_BLOCKS, C], BF16, name="w_gate_sb")
         w_ad_sb = held.tile([P, D_BLOCKS, C], BF16, name="w_ad_sb")
-        nc.sync.dma_start(x_sb[:], x.rearrange("(k p) n -> p k n", p=P))
-        nc.sync.dma_start(w_gate_sb[:], w_gate.rearrange("(k p) c -> p k c", p=P))
-        nc.sync.dma_start(w_ad_sb[:], w_ad.rearrange("(k p) c -> p k c", p=P))
+        nc.scalar.dma_start(x_sb[:], x.rearrange("(k p) n -> p k n", p=P))
+        nc.scalar.dma_start(w_gate_sb[:], w_gate.rearrange("(k p) c -> p k c", p=P))
+        nc.scalar.dma_start(w_ad_sb[:], w_ad.rearrange("(k p) c -> p k c", p=P))
 
         tw_sb = held.tile([P, N], F32, name="tw_sb")
-        nc.sync.dma_start(tw_sb[:], tw.to_broadcast([P, N]))
+        nc.scalar.dma_start(tw_sb[:], tw.to_broadcast([P, N]))
 
         windows = [held.tile([P, S], F32, name=f"window{cb}") for cb in range(C_BLOCKS)]
         for cb in range(C_BLOCKS):
-            nc.sync.dma_start(windows[cb][:], base[cb * P : (cb + 1) * P, :])
+            queues[cb % 2].dma_start(windows[cb][:], base[cb * P : (cb + 1) * P, :])
 
+        gates = [held.tile([P, N], F32, name=f"gate{cb}") for cb in range(C_BLOCKS)]
+        ups = [held.tile([P, N], F32, name=f"up{cb}") for cb in range(C_BLOCKS)]
         for cb in range(C_BLOCKS):
             channels = slice(cb * P, (cb + 1) * P)
-
-            gate_ps = psum.tile([P, N], F32, name="gate_ps")
-            up_ps = psum.tile([P, N], F32, name="up_ps")
+            gate_ps = psum.tile([P, N], F32, name=f"gate_ps{cb}")
+            up_ps = psum.tile([P, N], F32, name=f"up_ps{cb}")
             for k in range(D_BLOCKS):
                 nc.tensor.matmul(
                     gate_ps[:], w_gate_sb[:, k, channels], x_sb[:, k, :],
@@ -54,13 +55,9 @@ def tile_feedforward_kernel(tc, base, x, w_gate, w_ad, tw, offs, out):
                     up_ps[:], w_ad_sb[:, k, channels], x_sb[:, k, :],
                     start=(k == 0), stop=(k == D_BLOCKS - 1),
                 )
+            nc.scalar.activation(gates[cb][:], gate_ps[:], SILU)
+            nc.vector.scalar_tensor_tensor(ups[cb][:], up_ps[:], SCALING, tw_sb[:], MULT, MULT)
 
-            gate = work.tile([P, N], F32, name="gate")
-            nc.scalar.activation(gate[:], gate_ps[:], SILU)
-
-            up = work.tile([P, N], F32, name="up")
-            nc.vector.scalar_tensor_tensor(up[:], up_ps[:], SCALING, tw_sb[:], MULT, MULT)
-
-            nc.vector.tensor_tensor(windows[cb][:].indirect(offsets[:]), gate[:], up[:], MULT)
-
-            nc.sync.dma_start(out[channels, :], windows[cb][:])
+        for cb in range(C_BLOCKS):
+            nc.vector.tensor_tensor(windows[cb][:].indirect(offsets[:]), gates[cb][:], ups[cb][:], MULT)
+            queues[cb % 2].dma_start(out[cb * P : (cb + 1) * P, :], windows[cb][:])

@@ -17,34 +17,39 @@ FLOPS = 2 * 2 * D * C * N
 
 def tile_feedforward_kernel(tc, base, x, w_gate, w_ad, tw, offs, out):
     nc = tc.nc
-    queues = [nc.sync, nc.scalar]
     with (
         tc.tile_pool(name="held", bufs=1) as held,
-        tc.psum_pool(name="psum", bufs=1) as psum,
+        tc.psum_pool(name="psum", bufs=2) as psum,
     ):
         offsets = held.tile([P, N // 16], U16, name="offsets")
         nc.sync.dma_start(offsets[:], offs)
 
+        windows = [held.tile([P, S], F32, name=f"window{cb}") for cb in range(C_BLOCKS)]
+        for cb in range(C_BLOCKS):
+            nc.sync.dma_start(windows[cb][:], base[cb * P : (cb + 1) * P, :])
+
         x_sb = held.tile([P, D_BLOCKS, N], BF16, name="x_sb")
         w_gate_sb = held.tile([P, D_BLOCKS, C], BF16, name="w_gate_sb")
         w_ad_sb = held.tile([P, D_BLOCKS, C], BF16, name="w_ad_sb")
-        nc.scalar.dma_start(x_sb[:], x.rearrange("(k p) n -> p k n", p=P))
-        nc.scalar.dma_start(w_gate_sb[:], w_gate.rearrange("(k p) c -> p k c", p=P))
-        nc.scalar.dma_start(w_ad_sb[:], w_ad.rearrange("(k p) c -> p k c", p=P))
+        nc.scalar.dma_start(x_sb[:], x.rearrange("(p k) n -> p k n", k=D_BLOCKS))
+        nc.scalar.dma_start(w_gate_sb[:], w_gate.rearrange("(p k) c -> p k c", k=D_BLOCKS))
+        nc.scalar.dma_start(w_ad_sb[:], w_ad.rearrange("(p k) c -> p k c", k=D_BLOCKS))
 
-        tw_sb = held.tile([P, N], F32, name="tw_sb")
-        nc.scalar.dma_start(tw_sb[:], tw.to_broadcast([P, N]))
-
-        windows = [held.tile([P, S], F32, name=f"window{cb}") for cb in range(C_BLOCKS)]
-        for cb in range(C_BLOCKS):
-            queues[cb % 2].dma_start(windows[cb][:], base[cb * P : (cb + 1) * P, :])
+        tw_row = held.tile([1, N], F32, name="tw_row")
+        nc.scalar.dma_start(tw_row[:], tw)
+        ones = held.tile([1, P], F32, name="ones")
+        nc.vector.memset(ones[:], 1.0)
+        tw_ps = psum.tile([P, N], F32, name="tw_ps")
+        nc.tensor.matmul(tw_ps[:], ones[:], tw_row[:], start=True, stop=True)
+        tw_scaled = held.tile([P, N], F32, name="tw_scaled")
+        nc.scalar.mul(tw_scaled[:], tw_ps[:], SCALING)
 
         gates = [held.tile([P, N], F32, name=f"gate{cb}") for cb in range(C_BLOCKS)]
         ups = [held.tile([P, N], F32, name=f"up{cb}") for cb in range(C_BLOCKS)]
         for cb in range(C_BLOCKS):
             channels = slice(cb * P, (cb + 1) * P)
-            gate_ps = psum.tile([P, N], F32, name=f"gate_ps{cb}")
-            up_ps = psum.tile([P, N], F32, name=f"up_ps{cb}")
+            gate_ps = psum.tile([P, N], F32, name="gate_ps")
+            up_ps = psum.tile([P, N], F32, name="up_ps")
             for k in range(D_BLOCKS):
                 nc.tensor.matmul(
                     gate_ps[:], w_gate_sb[:, k, channels], x_sb[:, k, :],
@@ -56,8 +61,8 @@ def tile_feedforward_kernel(tc, base, x, w_gate, w_ad, tw, offs, out):
                     start=(k == 0), stop=(k == D_BLOCKS - 1),
                 )
             nc.scalar.activation(gates[cb][:], gate_ps[:], SILU)
-            nc.vector.scalar_tensor_tensor(ups[cb][:], up_ps[:], SCALING, tw_sb[:], MULT, MULT)
+            nc.vector.tensor_tensor(ups[cb][:], up_ps[:], tw_scaled[:], MULT)
 
         for cb in range(C_BLOCKS):
             nc.vector.tensor_tensor(windows[cb][:].indirect(offsets[:]), gates[cb][:], ups[cb][:], MULT)
-            queues[cb % 2].dma_start(out[cb * P : (cb + 1) * P, :], windows[cb][:])
+            nc.sync.dma_start(out[cb * P : (cb + 1) * P, :], windows[cb][:])

@@ -24,9 +24,8 @@ def tile_feedforward_kernel(tc, base, x, w_gate, w_ad, tw, offs, out):
         offsets = held.tile([P, N // 16], U16, name="offsets")
         nc.sync.dma_start(offsets[:], offs)
 
-        windows = [held.tile([P, S], F32, name=f"window{cb}") for cb in range(C_BLOCKS)]
-        for cb in range(C_BLOCKS):
-            nc.sync.dma_start(windows[cb][:], base[cb * P : (cb + 1) * P, :])
+        tw_row = held.tile([1, N], F32, name="tw_row")
+        nc.scalar.dma_start(tw_row[:], tw)
 
         x_sb = held.tile([P, D_BLOCKS, N], BF16, name="x_sb")
         w_gate_sb = held.tile([P, D_BLOCKS, C], BF16, name="w_gate_sb")
@@ -35,8 +34,10 @@ def tile_feedforward_kernel(tc, base, x, w_gate, w_ad, tw, offs, out):
         nc.scalar.dma_start(w_gate_sb[:], w_gate.rearrange("(p k) c -> p k c", k=D_BLOCKS))
         nc.scalar.dma_start(w_ad_sb[:], w_ad.rearrange("(p k) c -> p k c", k=D_BLOCKS))
 
-        tw_row = held.tile([1, N], F32, name="tw_row")
-        nc.scalar.dma_start(tw_row[:], tw)
+        windows = [held.tile([P, S], F32, name=f"window{cb}") for cb in range(C_BLOCKS)]
+        for cb in range(C_BLOCKS):
+            nc.sync.dma_start(windows[cb][:], base[cb * P : (cb + 1) * P, :])
+
         ones = held.tile([1, P], F32, name="ones")
         nc.vector.memset(ones[:], 1.0)
         tw_ps = psum.tile([P, N], F32, name="tw_ps")
@@ -44,8 +45,6 @@ def tile_feedforward_kernel(tc, base, x, w_gate, w_ad, tw, offs, out):
         tw_scaled = held.tile([P, N], F32, name="tw_scaled")
         nc.scalar.mul(tw_scaled[:], tw_ps[:], SCALING)
 
-        gates = [held.tile([P, N], F32, name=f"gate{cb}") for cb in range(C_BLOCKS)]
-        ups = [held.tile([P, N], F32, name=f"up{cb}") for cb in range(C_BLOCKS)]
         for cb in range(C_BLOCKS):
             channels = slice(cb * P, (cb + 1) * P)
             gate_ps = psum.tile([P, N], F32, name="gate_ps")
@@ -60,9 +59,10 @@ def tile_feedforward_kernel(tc, base, x, w_gate, w_ad, tw, offs, out):
                     up_ps[:], w_ad_sb[:, k, channels], x_sb[:, k, :],
                     start=(k == 0), stop=(k == D_BLOCKS - 1),
                 )
-            nc.scalar.activation(gates[cb][:], gate_ps[:], SILU)
-            nc.vector.tensor_tensor(ups[cb][:], up_ps[:], tw_scaled[:], MULT)
+            gate = held.tile([P, N], F32, name=f"gate{cb}")
+            nc.scalar.activation(gate[:], gate_ps[:], SILU)
+            up = held.tile([P, N], F32, name=f"up{cb}")
+            nc.vector.tensor_tensor(up[:], up_ps[:], tw_scaled[:], MULT)
 
-        for cb in range(C_BLOCKS):
-            nc.vector.tensor_tensor(windows[cb][:].indirect(offsets[:]), gates[cb][:], ups[cb][:], MULT)
-            nc.sync.dma_start(out[cb * P : (cb + 1) * P, :], windows[cb][:])
+            nc.vector.tensor_tensor(windows[cb][:].indirect(offsets[:]), gate[:], up[:], MULT)
+            nc.sync.dma_start(out[channels, :], windows[cb][:])

@@ -17,6 +17,7 @@ FLOPS = 2 * 2 * D * C * N
 
 def tile_feedforward_kernel(tc, base, x, w_gate, w_ad, tw, offs, out):
     nc = tc.nc
+    queues = [nc.sync, nc.scalar]
     with (
         tc.tile_pool(name="held", bufs=1) as held,
         tc.psum_pool(name="psum", bufs=2) as psum,
@@ -36,7 +37,7 @@ def tile_feedforward_kernel(tc, base, x, w_gate, w_ad, tw, offs, out):
 
         windows = [held.tile([P, S], F32, name=f"window{cb}") for cb in range(C_BLOCKS)]
         for cb in range(C_BLOCKS):
-            nc.sync.dma_start(windows[cb][:], base[cb * P : (cb + 1) * P, :])
+            queues[cb % 2].dma_start(windows[cb][:], base[cb * P : (cb + 1) * P, :])
 
         ones = held.tile([1, P], F32, name="ones")
         nc.vector.memset(ones[:], 1.0)
@@ -45,6 +46,8 @@ def tile_feedforward_kernel(tc, base, x, w_gate, w_ad, tw, offs, out):
         tw_scaled = held.tile([P, N], F32, name="tw_scaled")
         nc.scalar.mul(tw_scaled[:], tw_ps[:], SCALING)
 
+        gates = [held.tile([P, N], F32, name=f"gate{cb}") for cb in range(C_BLOCKS)]
+        ups = [held.tile([P, N], F32, name=f"up{cb}") for cb in range(C_BLOCKS)]
         for cb in range(C_BLOCKS):
             channels = slice(cb * P, (cb + 1) * P)
             gate_ps = psum.tile([P, N], F32, name="gate_ps")
@@ -59,10 +62,9 @@ def tile_feedforward_kernel(tc, base, x, w_gate, w_ad, tw, offs, out):
                     up_ps[:], w_ad_sb[:, k, channels], x_sb[:, k, :],
                     start=(k == 0), stop=(k == D_BLOCKS - 1),
                 )
-            gate = held.tile([P, N], F32, name=f"gate{cb}")
-            nc.scalar.activation(gate[:], gate_ps[:], SILU)
-            up = held.tile([P, N], F32, name=f"up{cb}")
-            nc.vector.tensor_tensor(up[:], up_ps[:], tw_scaled[:], MULT)
+            nc.scalar.activation(gates[cb][:], gate_ps[:], SILU)
+            nc.vector.tensor_tensor(ups[cb][:], up_ps[:], tw_scaled[:], MULT)
 
-            nc.vector.tensor_tensor(windows[cb][:].indirect(offsets[:]), gate[:], up[:], MULT)
-            nc.sync.dma_start(out[channels, :], windows[cb][:])
+        for cb in range(C_BLOCKS):
+            nc.vector.tensor_tensor(windows[cb][:].indirect(offsets[:]), gates[cb][:], ups[cb][:], MULT)
+            queues[cb % 2].dma_start(out[cb * P : (cb + 1) * P, :], windows[cb][:])

@@ -17,7 +17,6 @@ FLOPS = 2 * 2 * D * C * N
 
 def tile_feedforward_kernel(tc, base, x, w_gate, w_ad, tw, offs, out):
     nc = tc.nc
-    queues = [nc.sync, nc.scalar]
     with (
         tc.tile_pool(name="held", bufs=1) as held,
         tc.psum_pool(name="psum", bufs=2) as psum,
@@ -31,13 +30,13 @@ def tile_feedforward_kernel(tc, base, x, w_gate, w_ad, tw, offs, out):
         x_sb = held.tile([P, D_BLOCKS, N], BF16, name="x_sb")
         w_gate_sb = held.tile([P, D_BLOCKS, C], BF16, name="w_gate_sb")
         w_ad_sb = held.tile([P, D_BLOCKS, C], BF16, name="w_ad_sb")
-        nc.scalar.dma_start(x_sb[:], x.rearrange("(p k) n -> p k n", k=D_BLOCKS))
-        nc.scalar.dma_start(w_gate_sb[:], w_gate.rearrange("(p k) c -> p k c", k=D_BLOCKS))
-        nc.scalar.dma_start(w_ad_sb[:], w_ad.rearrange("(p k) c -> p k c", k=D_BLOCKS))
+        nc.sync.dma_start(x_sb[:], x.rearrange("(p k) n -> p k n", k=D_BLOCKS))
+        nc.sync.dma_start(w_gate_sb[:], w_gate.rearrange("(p k) c -> p k c", k=D_BLOCKS))
+        nc.sync.dma_start(w_ad_sb[:], w_ad.rearrange("(p k) c -> p k c", k=D_BLOCKS))
 
         windows = [held.tile([P, S], F32, name=f"window{cb}") for cb in range(C_BLOCKS)]
         for cb in range(C_BLOCKS):
-            queues[cb % 2].dma_start(windows[cb][:], base[cb * P : (cb + 1) * P, :])
+            nc.sync.dma_start(windows[cb][:], base[cb * P : (cb + 1) * P, :])
 
         ones = held.tile([1, P], F32, name="ones")
         nc.vector.memset(ones[:], 1.0)
@@ -67,4 +66,4 @@ def tile_feedforward_kernel(tc, base, x, w_gate, w_ad, tw, offs, out):
 
         for cb in range(C_BLOCKS):
             nc.vector.tensor_tensor(windows[cb][:].indirect(offsets[:]), gates[cb][:], ups[cb][:], MULT)
-            queues[cb % 2].dma_start(out[cb * P : (cb + 1) * P, :], windows[cb][:])
+            nc.sync.dma_start(out[cb * P : (cb + 1) * P, :], windows[cb][:])

@@ -45,8 +45,6 @@ def tile_feedforward_kernel(tc, base, x, w_gate, w_ad, tw, offs, out):
         tw_scaled = held.tile([P, N], F32, name="tw_scaled")
         nc.scalar.mul(tw_scaled[:], tw_ps[:], SCALING)
 
-        gates = [held.tile([P, N], F32, name=f"gate{cb}") for cb in range(C_BLOCKS)]
-        ups = [held.tile([P, N], F32, name=f"up{cb}") for cb in range(C_BLOCKS)]
         for cb in range(C_BLOCKS):
             channels = slice(cb * P, (cb + 1) * P)
             gate_ps = psum.tile([P, N], F32, name="gate_ps")
@@ -61,9 +59,9 @@ def tile_feedforward_kernel(tc, base, x, w_gate, w_ad, tw, offs, out):
                     up_ps[:], w_ad_sb[:, k, channels], x_sb[:, k, :],
                     start=(k == 0), stop=(k == D_BLOCKS - 1),
                 )
-            nc.scalar.activation(gates[cb][:], gate_ps[:], SILU)
-            nc.vector.tensor_tensor(ups[cb][:], up_ps[:], tw_scaled[:], MULT)
-
-        for cb in range(C_BLOCKS):
-            nc.vector.tensor_tensor(windows[cb][:].indirect(offsets[:]), gates[cb][:], ups[cb][:], MULT)
+            gate = held.tile([P, N], F32, name=f"gate{cb}")
+            up = held.tile([P, N], F32, name=f"up{cb}")
+            nc.scalar.activation(gate[:], gate_ps[:], SILU)
+            nc.vector.tensor_tensor(up[:], up_ps[:], tw_scaled[:], MULT)
+            nc.vector.tensor_tensor(windows[cb][:].indirect(offsets[:]), gate[:], up[:], MULT)
             nc.sync.dma_start(out[cb * P : (cb + 1) * P, :], windows[cb][:])

@@ -21,18 +21,18 @@ def tile_feedforward_kernel(tc, base, x, w_gate, w_ad, tw, offs, out):
         tc.tile_pool(name="held", bufs=1) as held,
         tc.psum_pool(name="psum", bufs=2) as psum,
     ):
-        offsets = held.tile([P, N // 16], U16, name="offsets")
-        nc.sync.dma_start(offsets[:], offs)
-
-        tw_row = held.tile([1, N], F32, name="tw_row")
-        nc.scalar.dma_start(tw_row[:], tw)
-
         x_sb = held.tile([P, D_BLOCKS, N], BF16, name="x_sb")
         w_gate_sb = held.tile([P, D_BLOCKS, C], BF16, name="w_gate_sb")
         w_ad_sb = held.tile([P, D_BLOCKS, C], BF16, name="w_ad_sb")
         nc.sync.dma_start(x_sb[:], x.rearrange("(p k) n -> p k n", k=D_BLOCKS))
         nc.sync.dma_start(w_gate_sb[:], w_gate.rearrange("(p k) c -> p k c", k=D_BLOCKS))
         nc.sync.dma_start(w_ad_sb[:], w_ad.rearrange("(p k) c -> p k c", k=D_BLOCKS))
+
+        tw_row = held.tile([1, N], F32, name="tw_row")
+        nc.sync.dma_start(tw_row[:], tw)
+
+        offsets = held.tile([P, N // 16], U16, name="offsets")
+        nc.sync.dma_start(offsets[:], offs)
 
         windows = [held.tile([P, S], F32, name=f"window{cb}") for cb in range(C_BLOCKS)]
         for cb in range(C_BLOCKS):

@@ -11,6 +11,7 @@ C, D, S, N = 512, 256, 2048, 256
 C_BLOCKS = C // P
 D_BLOCKS = D // P
 SCALING = 4.0
+BUS_ALIGN = 256
 
 FLOPS = 2 * 2 * D * C * N
 
@@ -21,9 +22,9 @@ def tile_feedforward_kernel(tc, base, x, w_gate, w_ad, tw, offs, out):
         tc.tile_pool(name="held", bufs=1) as held,
         tc.psum_pool(name="psum", bufs=2) as psum,
     ):
-        x_sb = held.tile([P, D_BLOCKS, N], BF16, name="x_sb")
-        w_gate_sb = held.tile([P, D_BLOCKS, C], BF16, name="w_gate_sb")
-        w_ad_sb = held.tile([P, D_BLOCKS, C], BF16, name="w_ad_sb")
+        x_sb = held.tile([P, D_BLOCKS, N], BF16, name="x_sb", align_bytes=BUS_ALIGN)
+        w_gate_sb = held.tile([P, D_BLOCKS, C], BF16, name="w_gate_sb", align_bytes=BUS_ALIGN)
+        w_ad_sb = held.tile([P, D_BLOCKS, C], BF16, name="w_ad_sb", align_bytes=BUS_ALIGN)
         nc.sync.dma_start(x_sb[:], x.rearrange("(p k) n -> p k n", k=D_BLOCKS))
         nc.sync.dma_start(w_gate_sb[:], w_gate.rearrange("(p k) c -> p k c", k=D_BLOCKS))
         nc.sync.dma_start(w_ad_sb[:], w_ad.rearrange("(p k) c -> p k c", k=D_BLOCKS))
@@ -34,7 +35,10 @@ def tile_feedforward_kernel(tc, base, x, w_gate, w_ad, tw, offs, out):
         offsets = held.tile([P, N // 16], U16, name="offsets")
         nc.sync.dma_start(offsets[:], offs)
 
-        windows = [held.tile([P, S], F32, name=f"window{cb}") for cb in range(C_BLOCKS)]
+        windows = [
+            held.tile([P, S], F32, name=f"window{cb}", align_bytes=BUS_ALIGN)
+            for cb in range(C_BLOCKS)
+        ]
         for cb in range(C_BLOCKS):
             nc.sync.dma_start(windows[cb][:], base[cb * P : (cb + 1) * P, :])
 

@@ -35,12 +35,14 @@ def tile_feedforward_kernel(tc, base, x, w_gate, w_ad, tw, offs, out):
         offsets = held.tile([P, N // 16], U16, name="offsets")
         nc.sync.dma_start(offsets[:], offs)
 
+        base_blocks = base.rearrange("(p b) s -> p b s", b=C_BLOCKS)
+        out_blocks = out.rearrange("(p b) s -> p b s", b=C_BLOCKS)
         windows = [
             held.tile([P, S], F32, name=f"window{cb}", align_bytes=BUS_ALIGN)
             for cb in range(C_BLOCKS)
         ]
         for cb in range(C_BLOCKS):
-            nc.sync.dma_start(windows[cb][:], base[cb * P : (cb + 1) * P, :])
+            nc.sync.dma_start(windows[cb][:], base_blocks[:, cb, :])
 
         ones = held.tile([1, P], F32, name="ones")
         nc.vector.memset(ones[:], 1.0)
@@ -50,7 +52,7 @@ def tile_feedforward_kernel(tc, base, x, w_gate, w_ad, tw, offs, out):
         nc.scalar.mul(tw_scaled[:], tw_ps[:], SCALING)
 
         for cb in range(C_BLOCKS):
-            channels = slice(cb * P, (cb + 1) * P)
+            channels = slice(cb, C, C_BLOCKS)
             gate_ps = psum.tile([P, N], F32, name="gate_ps")
             up_ps = psum.tile([P, N], F32, name="up_ps")
             for k in range(D_BLOCKS):
@@ -68,4 +70,4 @@ def tile_feedforward_kernel(tc, base, x, w_gate, w_ad, tw, offs, out):
             nc.scalar.activation(gate[:], gate_ps[:], SILU)
             nc.vector.tensor_tensor(up[:], up_ps[:], tw_scaled[:], MULT)
             nc.vector.tensor_tensor(windows[cb][:].indirect(offsets[:]), gate[:], up[:], MULT)
-            nc.sync.dma_start(out[cb * P : (cb + 1) * P, :], windows[cb][:])
+            nc.sync.dma_start(out_blocks[:, cb, :], windows[cb][:])

import concourse.mybir as mybir

F32 = mybir.dt.float32
BF16 = mybir.dt.bfloat16
U16 = mybir.dt.uint16
MULT = mybir.AluOpType.mult
SILU = mybir.ActivationFunctionType.Silu

P = 128
C, D, S, N = 512, 256, 2048, 256
C_BLOCKS = C // P
D_BLOCKS = D // P
SCALING = 4.0
BUS_ALIGN = 256

FLOPS = 2 * 2 * D * C * N


def tile_feedforward_kernel(tc, base, x, w_gate, w_ad, tw, offs, out):
    nc = tc.nc
    with (
        tc.tile_pool(name="held", bufs=1) as held,
        tc.psum_pool(name="psum", bufs=2) as psum,
    ):
        x_sb = held.tile([P, D_BLOCKS, N], BF16, name="x_sb", align_bytes=BUS_ALIGN)
        w_gate_sb = held.tile([P, D_BLOCKS, C], BF16, name="w_gate_sb", align_bytes=BUS_ALIGN)
        w_ad_sb = held.tile([P, D_BLOCKS, C], BF16, name="w_ad_sb", align_bytes=BUS_ALIGN)
        nc.sync.dma_start(x_sb[:], x.rearrange("(p k) n -> p k n", k=D_BLOCKS))
        nc.sync.dma_start(w_gate_sb[:], w_gate.rearrange("(p k) c -> p k c", k=D_BLOCKS))
        nc.sync.dma_start(w_ad_sb[:], w_ad.rearrange("(p k) c -> p k c", k=D_BLOCKS))

        tw_row = held.tile([1, N], F32, name="tw_row")
        nc.sync.dma_start(tw_row[:], tw)

        offsets = held.tile([P, N // 16], U16, name="offsets")
        nc.sync.dma_start(offsets[:], offs)

        base_blocks = base.rearrange("(p b) s -> p b s", b=C_BLOCKS)
        out_blocks = out.rearrange("(p b) s -> p b s", b=C_BLOCKS)
        windows = [
            held.tile([P, S], F32, name=f"window{cb}", align_bytes=BUS_ALIGN)
            for cb in range(C_BLOCKS)
        ]
        for cb in range(C_BLOCKS):
            nc.sync.dma_start(windows[cb][:], base_blocks[:, cb, :])

        ones = held.tile([1, P], F32, name="ones")
        nc.vector.memset(ones[:], 1.0)
        tw_ps = psum.tile([P, N], F32, name="tw_ps")
        nc.tensor.matmul(tw_ps[:], ones[:], tw_row[:], start=True, stop=True)
        tw_scaled = held.tile([P, N], F32, name="tw_scaled")
        nc.scalar.mul(tw_scaled[:], tw_ps[:], SCALING)

        for cb in range(C_BLOCKS):
            channels = slice(cb, C, C_BLOCKS)
            gate_ps = psum.tile([P, N], F32, name="gate_ps")
            up_ps = psum.tile([P, N], F32, name="up_ps")
            for k in range(D_BLOCKS):
                nc.tensor.matmul(
                    gate_ps[:], w_gate_sb[:, k, channels], x_sb[:, k, :],
                    start=(k == 0), stop=(k == D_BLOCKS - 1),
                )
            for k in range(D_BLOCKS):
                nc.tensor.matmul(
                    up_ps[:], w_ad_sb[:, k, channels], x_sb[:, k, :],
                    start=(k == 0), stop=(k == D_BLOCKS - 1),
                )
            gate = held.tile([P, N], F32, name=f"gate{cb}")
            up = held.tile([P, N], F32, name=f"up{cb}")
            nc.scalar.activation(gate[:], gate_ps[:], SILU)
            nc.vector.tensor_tensor(up[:], up_ps[:], tw_scaled[:], MULT)
            nc.vector.tensor_tensor(windows[cb][:].indirect(offsets[:]), gate[:], up[:], MULT)
            nc.sync.dma_start(out_blocks[:, cb, :], windows[cb][:])
